import numpy as np
import ml_dtypes


def mxq(x, axis, fmt="e4m3"):
    dtype, down = {"e4m3": (ml_dtypes.float8_e4m3fn, 7), "e5m2": (ml_dtypes.float8_e5m2, 14)}[fmt]
    v = np.moveaxis(np.asarray(x, np.float32).astype(ml_dtypes.bfloat16).astype(np.float64), axis, -1)
    blocks = v.reshape(v.shape[:-1] + (-1, 32))
    amax = np.abs(blocks).max(-1, keepdims=True)
    byte = np.maximum(np.where(amax > 0, np.frexp(amax)[1] - 1 + 127, 0) - down, 1)
    scale = np.exp2(byte - 127.0)
    codes = (blocks / scale).astype(np.float32).astype(dtype).astype(np.float64)
    return np.moveaxis((codes * scale).reshape(v.shape), -1, axis)


WIDE = False


def mx_kscale(k):
    if not WIDE:
        return np.ones(k)
    levels = np.array([10, -10, 5, -5, 0])
    a = np.random.permutation(np.resize(levels, k // 512 * 4)).reshape(k // 512, 4)
    idx = np.arange(k)
    return np.exp2(a[idx // 512, idx % 128 // 32])


BF16 = ml_dtypes.bfloat16


def bf(x):
    return np.asarray(x, np.float32).astype(BF16)


def f64(x):
    return np.asarray(x).astype(np.float64)


B, K, NH, N = 256, 1024, 512, 512
EPSILON = 0.1


def setup_inputs():
    s = mx_kscale(K)
    g = 1.0 / np.mean(1.0 / s)
    return {"x": bf(np.random.standard_normal((B, K)) * s),
            "y": bf(np.random.standard_normal((B, N)) * 12.0 / np.sqrt(K) * g),
            "beta": bf(np.random.random((K, N)) * 1.7 / np.sqrt(K) / s[:, None]),
            "bias_lin": bf(np.random.standard_normal(N) * 0.1),
            "W1": bf(-np.random.random((NH, K)) * 1.7 / np.sqrt(K) / s[None, :]),
            "W2": bf(np.random.random((N, NH)) * (0.5 + np.random.random((N, 1))) * 2.0 / NH**2),
            "bias1": bf(np.random.standard_normal(NH) * 0.1),
            "bias2": bf(np.random.standard_normal(N) * 0.1),
            "adv": 1}


def reference(x, y, beta, bias_lin, W1, W2, bias1, bias2, adv):
    xq = mxq(f64(x), 1, "e4m3")
    lin = (xq @ mxq(f64(beta), 0, "e4m3")) + f64(bias_lin)
    if adv:
        beta_norm = np.sum(np.abs(f64(beta)), axis=0)
        lin = lin - EPSILON * f64(y) * beta_norm
    if adv:
        one = NH * np.sum(f64(W2), axis=1) + f64(bias2)
        one = np.broadcast_to(one, lin.shape)
    else:
        h = np.maximum((xq @ mxq(f64(W1), 1, "e4m3").T) + f64(bias1), 0.0)
        one = (mxq(h, 1, "e4m3") @ mxq(f64(W2), 1, "e4m3").T) + f64(bias2)
    return lin + one

@@ -1,0 +1,174 @@
+from contextlib import ExitStack
+
+import concourse.mybir as mybir
+from concourse.masks import make_identity
+
+F32 = mybir.dt.float32
+BF16 = mybir.dt.bfloat16
+U32 = mybir.dt.uint32
+U8 = mybir.dt.uint8
+FP8X4 = mybir.dt.float8_e4m3fn_x4
+ALU = mybir.AluOpType
+ACT = mybir.ActivationFunctionType
+AXIS = mybir.AxisListType
+
+P = 128
+PACK = 4
+K_PASS = P * PACK
+B, K, N, NH = 256, 1024, 512, 512
+PASSES = K // K_PASS
+ROW_TILES = B // P
+COL_TILES = N // P
+EPSILON = 0.1
+
+VECTOR_COLS = 320
+
+FLOPS = 2 * B * K * N
+BYTES = 2 * (B * K + B * N + K * N + N * NH + 2 * N) + 4 * B * N
+
+
+def tile_advresnet_s_kernel(tc, x, y, beta, bias_lin, W1, W2, bias1, bias2, adv, out):
+    assert adv == 1
+    nc = tc.nc
+    with ExitStack() as ctx:
+        keep = ctx.enter_context(tc.tile_pool(name="keep", bufs=1))
+        psum = ctx.enter_context(tc.psum_pool(name="psum", bufs=1))
+
+        ident = keep.tile([P, P], F32)
+        make_identity(nc, ident[:])
+        weight = keep.tile([P, 2], BF16)
+        nc.vector.memset(weight[:, 0:1], -1.0)
+        nc.vector.memset(weight[:, 1:2], 2.0)
+
+        bias_lin_sb = keep.tile([P, COL_TILES], BF16)
+        bias2_sb = keep.tile([P, COL_TILES], BF16)
+        nc.scalar.dma_start(out=bias_lin_sb[:], in_=bias_lin.rearrange("(p t) -> p t", p=P))
+        nc.scalar.dma_start(out=bias2_sb[:], in_=bias2.rearrange("(p t) -> p t", p=P))
+
+        beta_sb = keep.tile([P, PASSES, PACK, N], BF16)
+        for g in range(PASSES):
+            nc.sync.dma_start(
+                out=beta_sb[:, g].rearrange("p (u e) n -> p u (e n)", u=2),
+                in_=beta[g * K_PASS : (g + 1) * K_PASS, :].rearrange("(u p e) n -> p u (e n)", u=2, e=2),
+            )
+        x_sb = keep.tile([P, ROW_TILES * K], BF16)
+        nc.sync.dma_start(
+            out=x_sb[:].rearrange("p (r k) -> p r k", r=ROW_TILES),
+            in_=x.rearrange("(r p) k -> p r k", p=P),
+        )
+        w2_sb = keep.tile([P, COL_TILES, NH], BF16)
+        nc.sync.dma_start(out=w2_sb[:], in_=W2.rearrange("(p t) h -> p t h", p=P))
+        y_sb = keep.tile([P, ROW_TILES, N], BF16)
+        nc.sync.dma_start(out=y_sb[:], in_=y.rearrange("(r p) n -> p r n", p=P))
+
+        beta_pos = keep.tile([P, PASSES, PACK, N], BF16)
+        beta_grouped = keep.tile([P, PASSES, N, PACK], BF16, align_bytes=64)
+        beta_codes = keep.tile([P, PASSES, N], U32, align_bytes=64)
+        beta_scales = keep.tile([P, PASSES, N], U8, align_bytes=64)
+        norm_ps = psum.tile([P, COL_TILES, 2 * PASSES], F32)
+        for g in range(PASSES):
+            nc.vector.tensor_scalar_max(out=beta_pos[:, g], in0=beta_sb[:, g], scalar1=0.0)
+            src = beta_sb[:, g].rearrange("p t (c i) -> p c t i", i=4)
+            dst = beta_grouped[:, g].rearrange("p (c i) t -> p c t i", i=4)
+            cut = VECTOR_COLS // 4
+            nc.vector.tensor_copy(out=dst[:, :cut], in_=src[:, :cut])
+            nc.scalar.copy(out=dst[:, cut:], in_=src[:, cut:])
+            for part, source in enumerate((beta_sb, beta_pos)):
+                for j in range(COL_TILES):
+                    for t in range(PACK):
+                        nc.tensor.matmul(
+                            out=norm_ps[:, j, 2 * g + part : 2 * g + part + 1],
+                            lhsT=source[:, g, t, j * P : (j + 1) * P],
+                            rhs=weight[:, part : part + 1],
+                            start=(t == 0),
+                            stop=(t == PACK - 1),
+                        )
+        for g in range(PASSES):
+            nc.vector.quantize_mx(
+                out=beta_codes[:, g].bitcast(FP8X4),
+                scales=beta_scales[:, g],
+                in_=beta_grouped[:, g].rearrange("p n t -> p (n t)"),
+            )
+
+        x_words = x_sb[:].bitcast(F32).rearrange("p (r w) -> p r w", r=ROW_TILES)
+        x_grouped = keep.tile([P, PASSES * B * PACK], BF16, align_bytes=64)
+        x_grouped_words = x_grouped[:].bitcast(F32).rearrange("p (g row u) -> p g row u", g=PASSES, u=2)
+        x_codes = keep.tile([P, PASSES * B], U32, align_bytes=64)
+        x_scales = keep.tile([P, PASSES * B], U8, align_bytes=64)
+        for g in range(PASSES):
+            xt = psum.tile([P, 2, B], F32, name="xt%d" % g)
+            for u in range(2):
+                for r in range(ROW_TILES):
+                    first_word = (2 * g + u) * P
+                    nc.tensor.transpose(
+                        xt[:, u, r * P : (r + 1) * P],
+                        x_words[:, r, first_word : first_word + P],
+                        ident[:],
+                    )
+            nc.scalar.copy(out=x_grouped_words[:, g], in_=xt[:].rearrange("p u row -> p row u"))
+        nc.vector.quantize_mx(out=x_codes[:].bitcast(FP8X4), scales=x_scales[:], in_=x_grouped[:])
+
+        norm_sb = keep.tile([P, COL_TILES], F32)
+        nc.vector.tensor_reduce(out=norm_sb[:], in_=norm_ps[:], axis=AXIS.X, op=ALU.add)
+        norm_rows = psum.tile([P, N], F32)
+        for j in range(COL_TILES):
+            nc.tensor.transpose(
+                norm_rows[:, j * P : (j + 1) * P],
+                norm_sb[:, j : j + 1].to_broadcast([P, P]),
+                ident[:],
+            )
+
+        bias_sum = keep.tile([P, COL_TILES], F32)
+        nc.gpsimd.tensor_tensor(out=bias_sum[:], in0=bias_lin_sb[:], in1=bias2_sb[:], op=ALU.add)
+        w2_scaled = keep.tile([P, COL_TILES, NH], BF16)
+        w2_sums = keep.tile([P, COL_TILES], F32)
+        for t in range(COL_TILES):
+            nc.scalar.activation(
+                out=w2_scaled[:, t],
+                in_=w2_sb[:, t],
+                func=ACT.Copy,
+                scale=float(NH),
+                accum_out=w2_sums[:, t : t + 1],
+            )
+        shift_sb = keep.tile([P, COL_TILES], F32)
+        nc.gpsimd.tensor_tensor(out=shift_sb[:], in0=w2_sums[:], in1=bias_sum[:], op=ALU.add)
+        shift_rows = psum.tile([P, COL_TILES, P], F32)
+        for t in range(COL_TILES):
+            nc.tensor.transpose(
+                shift_rows[:, t, :],
+                shift_sb[:, t : t + 1].to_broadcast([P, P]),
+                ident[:],
+            )
+
+        rest = keep.tile([P, ROW_TILES, N], F32)
+        for r in range(ROW_TILES):
+            nc.vector.scalar_tensor_tensor(
+                out=rest[:, r],
+                in0=y_sb[:, r],
+                scalar=-EPSILON,
+                in1=norm_rows[:],
+                op0=ALU.mult,
+                op1=ALU.mult,
+            )
+        for r in range(ROW_TILES):
+            rest_qt = rest[:, r].rearrange("p (q t) -> p q t", t=COL_TILES)
+            nc.vector.tensor_tensor(
+                out=rest_qt, in0=rest_qt, in1=shift_rows[:].rearrange("p t q -> p q t"), op=ALU.add
+            )
+
+        result = keep.tile([P, ROW_TILES, N], F32)
+        for r in range(ROW_TILES):
+            acc = psum.tile([P, N], F32, name="acc%d" % r)
+            for g in range(PASSES):
+                rows = slice(g * B + r * P, g * B + (r + 1) * P)
+                nc.tensor.matmul_mx(
+                    out=acc[:],
+                    lhsT=x_codes[:, rows].bitcast(FP8X4),
+                    lhsT_scale=x_scales[:, rows],
+                    rhs=beta_codes[:, g].bitcast(FP8X4),
+                    rhs_scale=beta_scales[:, g],
+                    start=(g == 0),
+                    stop=(g == PASSES - 1),
+                )
+            nc.vector.tensor_tensor(out=result[:, r], in0=rest[:, r], in1=acc[:], op=ALU.add)
+            nc.sync.dma_start(out=out[r * P : (r + 1) * P, :], in_=result[:, r])

@@ -33,24 +33,16 @@ def tile_advresnet_s_kernel(tc, x, y, beta, bias_lin, W1, W2, bias1, bias2, adv,
     with ExitStack() as ctx:
         keep = ctx.enter_context(tc.tile_pool(name="keep", bufs=1))
         psum = ctx.enter_context(tc.psum_pool(name="psum", bufs=1))
-
-        ident = keep.tile([P, P], F32)
-        make_identity(nc, ident[:])
-        weight = keep.tile([P, 2], BF16)
-        nc.vector.memset(weight[:, 0:1], -1.0)
-        nc.vector.memset(weight[:, 1:2], 2.0)
-
-        bias_lin_sb = keep.tile([P, COL_TILES], BF16)
-        bias2_sb = keep.tile([P, COL_TILES], BF16)
-        nc.scalar.dma_start(out=bias_lin_sb[:], in_=bias_lin.rearrange("(p t) -> p t", p=P))
-        nc.scalar.dma_start(out=bias2_sb[:], in_=bias2.rearrange("(p t) -> p t", p=P))
+        ctx.enter_context(tc.manual_schedule())
 
         beta_sb = keep.tile([P, PASSES, PACK, N], BF16)
         for g in range(PASSES):
-            nc.sync.dma_start(
-                out=beta_sb[:, g].rearrange("p (u e) n -> p u (e n)", u=2),
-                in_=beta[g * K_PASS : (g + 1) * K_PASS, :].rearrange("(u p e) n -> p u (e n)", u=2, e=2),
-            )
+            for u in range(2):
+                first_row = g * K_PASS + u * 2 * P
+                nc.sync.dma_start(
+                    out=beta_sb[:, g, 2 * u : 2 * u + 2, :].rearrange("p e n -> p (e n)"),
+                    in_=beta[first_row : first_row + 2 * P, :].rearrange("(p e) n -> p (e n)", e=2),
+                )
         x_sb = keep.tile([P, ROW_TILES * K], BF16)
         nc.sync.dma_start(
             out=x_sb[:].rearrange("p (r k) -> p r k", r=ROW_TILES),
@@ -60,14 +52,29 @@ def tile_advresnet_s_kernel(tc, x, y, beta, bias_lin, W1, W2, bias1, bias2, adv,
         nc.sync.dma_start(out=w2_sb[:], in_=W2.rearrange("(p t) h -> p t h", p=P))
         y_sb = keep.tile([P, ROW_TILES, N], BF16)
         nc.sync.dma_start(out=y_sb[:], in_=y.rearrange("(r p) n -> p r n", p=P))
+        bias_lin_sb = keep.tile([P, COL_TILES], BF16)
+        bias2_sb = keep.tile([P, COL_TILES], BF16)
+        nc.scalar.dma_start(out=bias_lin_sb[:], in_=bias_lin.rearrange("(p t) -> p t", p=P))
+        nc.scalar.dma_start(out=bias2_sb[:], in_=bias2.rearrange("(p t) -> p t", p=P))
+
+        ident = keep.tile([P, P], F32)
+        make_identity(nc, ident[:])
+        weight = keep.tile([P, 2], BF16)
+        nc.vector.memset(weight[:, 0:1], -1.0)
+        nc.vector.memset(weight[:, 1:2], 2.0)
+        table_warmer = keep.tile([P, 1], BF16)
+        nc.scalar.copy(out=table_warmer[:], in_=weight[:, 0:1])
 
         beta_pos = keep.tile([P, PASSES, PACK, N], BF16)
         beta_grouped = keep.tile([P, PASSES, N, PACK], BF16, align_bytes=64)
-        beta_codes = keep.tile([P, PASSES, N], U32, align_bytes=64)
-        beta_scales = keep.tile([P, PASSES, N], U8, align_bytes=64)
         norm_ps = psum.tile([P, COL_TILES, 2 * PASSES], F32)
         for g in range(PASSES):
-            nc.vector.tensor_scalar_max(out=beta_pos[:, g], in0=beta_sb[:, g], scalar1=0.0)
+            for u in range(2):
+                nc.vector.tensor_scalar_max(
+                    out=beta_pos[:, g, 2 * u : 2 * u + 2, :],
+                    in0=beta_sb[:, g, 2 * u : 2 * u + 2, :],
+                    scalar1=0.0,
+                )
             src = beta_sb[:, g].rearrange("p t (c i) -> p c t i", i=4)
             dst = beta_grouped[:, g].rearrange("p (c i) t -> p c t i", i=4)
             cut = VECTOR_COLS // 4
@@ -83,12 +90,18 @@ def tile_advresnet_s_kernel(tc, x, y, beta, bias_lin, W1, W2, bias1, bias2, adv,
                             start=(t == 0),
                             stop=(t == PACK - 1),
                         )
+
+        beta_codes = keep.tile([P, PASSES, N], U32, align_bytes=64)
+        beta_scales = keep.tile([P, PASSES, N], U8, align_bytes=64)
+        norm_sb = keep.tile([P, COL_TILES], F32)
         for g in range(PASSES):
             nc.vector.quantize_mx(
                 out=beta_codes[:, g].bitcast(FP8X4),
                 scales=beta_scales[:, g],
                 in_=beta_grouped[:, g].rearrange("p n t -> p (n t)"),
             )
+            if g == 0:
+                nc.vector.tensor_reduce(out=norm_sb[:], in_=norm_ps[:], axis=AXIS.X, op=ALU.add)
 
         x_words = x_sb[:].bitcast(F32).rearrange("p (r w) -> p r w", r=ROW_TILES)
         x_grouped = keep.tile([P, PASSES * B * PACK], BF16, align_bytes=64)
@@ -106,10 +119,13 @@ def tile_advresnet_s_kernel(tc, x, y, beta, bias_lin, W1, W2, bias1, bias2, adv,
                         ident[:],
                     )
             nc.scalar.copy(out=x_grouped_words[:, g], in_=xt[:].rearrange("p u row -> p row u"))
-        nc.vector.quantize_mx(out=x_codes[:].bitcast(FP8X4), scales=x_scales[:], in_=x_grouped[:])
+        for g in range(PASSES):
+            nc.vector.quantize_mx(
+                out=x_codes[:, g * B : (g + 1) * B].bitcast(FP8X4),
+                scales=x_scales[:, g * B : (g + 1) * B],
+                in_=x_grouped[:, g * B * PACK : (g + 1) * B * PACK],
+            )
 
-        norm_sb = keep.tile([P, COL_TILES], F32)
-        nc.vector.tensor_reduce(out=norm_sb[:], in_=norm_ps[:], axis=AXIS.X, op=ALU.add)
         norm_rows = psum.tile([P, N], F32)
         for j in range(COL_TILES):
             nc.tensor.transpose(
@@ -117,6 +133,20 @@ def tile_advresnet_s_kernel(tc, x, y, beta, bias_lin, W1, W2, bias1, bias2, adv,
                 norm_sb[:, j : j + 1].to_broadcast([P, P]),
                 ident[:],
             )
+
+        acc = [psum.tile([P, N], F32, name="acc%d" % r) for r in range(ROW_TILES)]
+        for g in range(PASSES):
+            for r in range(ROW_TILES):
+                rows = slice(g * B + r * P, g * B + (r + 1) * P)
+                nc.tensor.matmul_mx(
+                    out=acc[r][:],
+                    lhsT=x_codes[:, rows].bitcast(FP8X4),
+                    lhsT_scale=x_scales[:, rows],
+                    rhs=beta_codes[:, g].bitcast(FP8X4),
+                    rhs_scale=beta_scales[:, g],
+                    start=(g == 0),
+                    stop=(g == PASSES - 1),
+                )
 
         bias_sum = keep.tile([P, COL_TILES], F32)
         nc.gpsimd.tensor_tensor(out=bias_sum[:], in0=bias_lin_sb[:], in1=bias2_sb[:], op=ALU.add)
@@ -130,20 +160,11 @@ def tile_advresnet_s_kernel(tc, x, y, beta, bias_lin, W1, W2, bias1, bias2, adv,
                 scale=float(NH),
                 accum_out=w2_sums[:, t : t + 1],
             )
-        shift_sb = keep.tile([P, COL_TILES], F32)
-        nc.gpsimd.tensor_tensor(out=shift_sb[:], in0=w2_sums[:], in1=bias_sum[:], op=ALU.add)
-        shift_rows = psum.tile([P, COL_TILES, P], F32)
-        for t in range(COL_TILES):
-            nc.tensor.transpose(
-                shift_rows[:, t, :],
-                shift_sb[:, t : t + 1].to_broadcast([P, P]),
-                ident[:],
-            )
 
-        rest = keep.tile([P, ROW_TILES, N], F32)
+        total = keep.tile([P, ROW_TILES, N], F32)
         for r in range(ROW_TILES):
             nc.vector.scalar_tensor_tensor(
-                out=rest[:, r],
+                out=total[:, r],
                 in0=y_sb[:, r],
                 scalar=-EPSILON,
                 in1=norm_rows[:],
@@ -151,24 +172,19 @@ def tile_advresnet_s_kernel(tc, x, y, beta, bias_lin, W1, W2, bias1, bias2, adv,
                 op1=ALU.mult,
             )
         for r in range(ROW_TILES):
-            rest_qt = rest[:, r].rearrange("p (q t) -> p q t", t=COL_TILES)
-            nc.vector.tensor_tensor(
-                out=rest_qt, in0=rest_qt, in1=shift_rows[:].rearrange("p t q -> p q t"), op=ALU.add
+            nc.vector.tensor_tensor(out=total[:, r], in0=total[:, r], in1=acc[r][:], op=ALU.add)
+        shift_sb = keep.tile([P, COL_TILES], F32)
+        nc.vector.tensor_tensor(out=shift_sb[:], in0=w2_sums[:], in1=bias_sum[:], op=ALU.add)
+        shift_rows = psum.tile([P, COL_TILES, P], F32)
+        for t in range(COL_TILES):
+            nc.tensor.transpose(
+                shift_rows[:, t, :],
+                shift_sb[:, t : t + 1].to_broadcast([P, P]),
+                ident[:],
             )
-
-        result = keep.tile([P, ROW_TILES, N], F32)
         for r in range(ROW_TILES):
-            acc = psum.tile([P, N], F32, name="acc%d" % r)
-            for g in range(PASSES):
-                rows = slice(g * B + r * P, g * B + (r + 1) * P)
-                nc.tensor.matmul_mx(
-                    out=acc[:],
-                    lhsT=x_codes[:, rows].bitcast(FP8X4),
-                    lhsT_scale=x_scales[:, rows],
-                    rhs=beta_codes[:, g].bitcast(FP8X4),
-                    rhs_scale=beta_scales[:, g],
-                    start=(g == 0),
-                    stop=(g == PASSES - 1),
-                )
-            nc.vector.tensor_tensor(out=result[:, r], in0=rest[:, r], in1=acc[:], op=ALU.add)
-            nc.sync.dma_start(out=out[r * P : (r + 1) * P, :], in_=result[:, r])
+            total_qt = total[:, r].rearrange("p (q t) -> p q t", t=COL_TILES)
+            nc.vector.tensor_tensor(
+                out=total_qt, in0=total_qt, in1=shift_rows[:].rearrange("p t q -> p q t"), op=ALU.add
+            )
+            nc.sync.dma_start(out=out[r * P : (r + 1) * P, :], in_=total[:, r])

@@ -21,7 +21,7 @@ ROW_TILES = B // P
 COL_TILES = N // P
 EPSILON = 0.1
 
-VECTOR_COLS = 320
+VECTOR_COLS = 256
 
 FLOPS = 2 * B * K * N
 BYTES = 2 * (B * K + B * N + K * N + N * NH + 2 * N) + 4 * B * N
@@ -148,17 +148,21 @@ def tile_advresnet_s_kernel(tc, x, y, beta, bias_lin, W1, W2, bias1, bias2, adv,
                     stop=(g == PASSES - 1),
                 )
 
-        bias_sum = keep.tile([P, COL_TILES], F32)
-        nc.gpsimd.tensor_tensor(out=bias_sum[:], in0=bias_lin_sb[:], in1=bias2_sb[:], op=ALU.add)
-        w2_scaled = keep.tile([P, COL_TILES, NH], BF16)
-        w2_sums = keep.tile([P, COL_TILES], F32)
+        bias_share = keep.tile([P, COL_TILES], F32)
+        nc.gpsimd.tensor_tensor(out=bias_share[:], in0=bias_lin_sb[:], in1=bias2_sb[:], op=ALU.add)
+        nc.gpsimd.tensor_scalar(
+            out=bias_share[:], in0=bias_share[:], scalar1=1.0 / NH, scalar2=0.0, op0=ALU.mult, op1=ALU.add
+        )
+        summands = keep.tile([P, COL_TILES, NH], BF16)
+        shift_sb = keep.tile([P, COL_TILES], F32)
         for t in range(COL_TILES):
             nc.scalar.activation(
-                out=w2_scaled[:, t],
+                out=summands[:, t],
                 in_=w2_sb[:, t],
-                func=ACT.Copy,
+                func=ACT.Identity,
                 scale=float(NH),
-                accum_out=w2_sums[:, t : t + 1],
+                bias=bias_share[:, t : t + 1],
+                accum_out=shift_sb[:, t : t + 1],
             )
 
         total = keep.tile([P, ROW_TILES, N], F32)
@@ -173,8 +177,6 @@ def tile_advresnet_s_kernel(tc, x, y, beta, bias_lin, W1, W2, bias1, bias2, adv,
             )
         for r in range(ROW_TILES):
             nc.vector.tensor_tensor(out=total[:, r], in0=total[:, r], in1=acc[r][:], op=ALU.add)
-        shift_sb = keep.tile([P, COL_TILES], F32)
-        nc.vector.tensor_tensor(out=shift_sb[:], in0=w2_sums[:], in1=bias_sum[:], op=ALU.add)
         shift_rows = psum.tile([P, COL_TILES, P], F32)
         for t in range(COL_TILES):
             nc.tensor.transpose(

@@ -118,7 +118,10 @@ def tile_advresnet_s_kernel(tc, x, y, beta, bias_lin, W1, W2, bias1, bias2, adv,
                         x_words[:, r, first_word : first_word + P],
                         ident[:],
                     )
-            nc.scalar.copy(out=x_grouped_words[:, g], in_=xt[:].rearrange("p u row -> p row u"))
+            if g == 0:
+                nc.scalar.copy(out=x_grouped_words[:, g], in_=xt[:].rearrange("p u row -> p row u"))
+            else:
+                nc.vector.tensor_copy(out=x_grouped_words[:, g], in_=xt[:].rearrange("p u row -> p row u"))
         for g in range(PASSES):
             nc.vector.quantize_mx(
                 out=x_codes[:, g * B : (g + 1) * B].bitcast(FP8X4),

@@ -14,11 +14,15 @@ AXIS = mybir.AxisListType
 
 P = 128
 PACK = 4
+PAIR = 2
+HALVES = PACK // PAIR
 K_PASS = P * PACK
 B, K, N, NH = 256, 1024, 512, 512
 PASSES = K // K_PASS
 ROW_TILES = B // P
 COL_TILES = N // P
+W2_ROWS = N // P
+RUN = 4
 EPSILON = 0.1
 
 VECTOR_COLS = 256
@@ -37,47 +41,45 @@ def tile_advresnet_s_kernel(tc, x, y, beta, bias_lin, W1, W2, bias1, bias2, adv,
 
         beta_sb = keep.tile([P, PASSES, PACK, N], BF16)
         for g in range(PASSES):
-            for u in range(2):
-                first_row = g * K_PASS + u * 2 * P
+            for u in range(HALVES):
+                first_row = g * K_PASS + u * PAIR * P
                 nc.sync.dma_start(
-                    out=beta_sb[:, g, 2 * u : 2 * u + 2, :].rearrange("p e n -> p (e n)"),
-                    in_=beta[first_row : first_row + 2 * P, :].rearrange("(p e) n -> p (e n)", e=2),
+                    out=beta_sb[:, g, PAIR * u : PAIR * (u + 1), :].rearrange("p e n -> p (e n)"),
+                    in_=beta[first_row : first_row + PAIR * P, :].rearrange("(p e) n -> p (e n)", e=PAIR),
                 )
         x_sb = keep.tile([P, ROW_TILES * K], BF16)
         nc.sync.dma_start(
             out=x_sb[:].rearrange("p (r k) -> p r k", r=ROW_TILES),
             in_=x.rearrange("(r p) k -> p r k", p=P),
         )
-        w2_sb = keep.tile([P, COL_TILES, NH], BF16)
-        nc.sync.dma_start(out=w2_sb[:], in_=W2.rearrange("(p t) h -> p t h", p=P))
+        w2_sb = keep.tile([P, W2_ROWS, NH], BF16)
+        nc.sync.dma_start(out=w2_sb[:], in_=W2.rearrange("(p i) h -> p i h", p=P))
         y_sb = keep.tile([P, ROW_TILES, N], BF16)
         nc.sync.dma_start(out=y_sb[:], in_=y.rearrange("(r p) n -> p r n", p=P))
-        bias_lin_sb = keep.tile([P, COL_TILES], BF16)
-        bias2_sb = keep.tile([P, COL_TILES], BF16)
-        nc.scalar.dma_start(out=bias_lin_sb[:], in_=bias_lin.rearrange("(p t) -> p t", p=P))
-        nc.scalar.dma_start(out=bias2_sb[:], in_=bias2.rearrange("(p t) -> p t", p=P))
+        bias_lin_sb = keep.tile([P, W2_ROWS], BF16)
+        bias2_sb = keep.tile([P, W2_ROWS], BF16)
+        nc.scalar.dma_start(out=bias_lin_sb[:], in_=bias_lin.rearrange("(p i) -> p i", p=P))
+        nc.scalar.dma_start(out=bias2_sb[:], in_=bias2.rearrange("(p i) -> p i", p=P))
 
         ident = keep.tile([P, P], F32)
         make_identity(nc, ident[:])
         weight = keep.tile([P, 2], BF16)
         nc.vector.memset(weight[:, 0:1], -1.0)
         nc.vector.memset(weight[:, 1:2], 2.0)
-        table_warmer = keep.tile([P, 1], BF16)
-        nc.scalar.copy(out=table_warmer[:], in_=weight[:, 0:1])
 
         beta_pos = keep.tile([P, PASSES, PACK, N], BF16)
         beta_grouped = keep.tile([P, PASSES, N, PACK], BF16, align_bytes=64)
         norm_ps = psum.tile([P, COL_TILES, 2 * PASSES], F32)
         for g in range(PASSES):
-            for u in range(2):
+            for u in range(HALVES):
                 nc.vector.tensor_scalar_max(
-                    out=beta_pos[:, g, 2 * u : 2 * u + 2, :],
-                    in0=beta_sb[:, g, 2 * u : 2 * u + 2, :],
+                    out=beta_pos[:, g, PAIR * u : PAIR * (u + 1), :],
+                    in0=beta_sb[:, g, PAIR * u : PAIR * (u + 1), :],
                     scalar1=0.0,
                 )
-            src = beta_sb[:, g].rearrange("p t (c i) -> p c t i", i=4)
-            dst = beta_grouped[:, g].rearrange("p (c i) t -> p c t i", i=4)
-            cut = VECTOR_COLS // 4
+            src = beta_sb[:, g].rearrange("p t (c i) -> p c t i", i=RUN)
+            dst = beta_grouped[:, g].rearrange("p (c i) t -> p c t i", i=RUN)
+            cut = VECTOR_COLS // RUN
             nc.vector.tensor_copy(out=dst[:, :cut], in_=src[:, :cut])
             nc.scalar.copy(out=dst[:, cut:], in_=src[:, cut:])
             for part, source in enumerate((beta_sb, beta_pos)):
@@ -94,34 +96,36 @@ def tile_advresnet_s_kernel(tc, x, y, beta, bias_lin, W1, W2, bias1, bias2, adv,
         beta_codes = keep.tile([P, PASSES, N], U32, align_bytes=64)
         beta_scales = keep.tile([P, PASSES, N], U8, align_bytes=64)
         norm_sb = keep.tile([P, COL_TILES], F32)
-        for g in range(PASSES):
+
+        def quantise_beta(g):
             nc.vector.quantize_mx(
                 out=beta_codes[:, g].bitcast(FP8X4),
                 scales=beta_scales[:, g],
                 in_=beta_grouped[:, g].rearrange("p n t -> p (n t)"),
             )
-            if g == 0:
-                nc.vector.tensor_reduce(out=norm_sb[:], in_=norm_ps[:], axis=AXIS.X, op=ALU.add)
+
+        quantise_beta(0)
+        nc.vector.tensor_reduce(out=norm_sb[:], in_=norm_ps[:], axis=AXIS.X, op=ALU.add)
+        quantise_beta(1)
 
         x_words = x_sb[:].bitcast(F32).rearrange("p (r w) -> p r w", r=ROW_TILES)
         x_grouped = keep.tile([P, PASSES * B * PACK], BF16, align_bytes=64)
-        x_grouped_words = x_grouped[:].bitcast(F32).rearrange("p (g row u) -> p g row u", g=PASSES, u=2)
+        x_grouped_words = x_grouped[:].bitcast(F32).rearrange(
+            "p (g row u) -> p g row u", g=PASSES, u=HALVES
+        )
         x_codes = keep.tile([P, PASSES * B], U32, align_bytes=64)
         x_scales = keep.tile([P, PASSES * B], U8, align_bytes=64)
         for g in range(PASSES):
-            xt = psum.tile([P, 2, B], F32, name="xt%d" % g)
-            for u in range(2):
+            xt = psum.tile([P, HALVES, B], F32, name="xt%d" % g)
+            for u in range(HALVES):
                 for r in range(ROW_TILES):
-                    first_word = (2 * g + u) * P
+                    first_word = (HALVES * g + u) * P
                     nc.tensor.transpose(
                         xt[:, u, r * P : (r + 1) * P],
                         x_words[:, r, first_word : first_word + P],
                         ident[:],
                     )
-            if g == 0:
-                nc.scalar.copy(out=x_grouped_words[:, g], in_=xt[:].rearrange("p u row -> p row u"))
-            else:
-                nc.vector.tensor_copy(out=x_grouped_words[:, g], in_=xt[:].rearrange("p u row -> p row u"))
+            nc.scalar.copy(out=x_grouped_words[:, g], in_=xt[:].rearrange("p u row -> p row u"))
         for g in range(PASSES):
             nc.vector.quantize_mx(
                 out=x_codes[:, g * B : (g + 1) * B].bitcast(FP8X4),
@@ -151,21 +155,21 @@ def tile_advresnet_s_kernel(tc, x, y, beta, bias_lin, W1, W2, bias1, bias2, adv,
                     stop=(g == PASSES - 1),
                 )
 
-        bias_share = keep.tile([P, COL_TILES], F32)
+        bias_share = keep.tile([P, W2_ROWS], F32)
         nc.gpsimd.tensor_tensor(out=bias_share[:], in0=bias_lin_sb[:], in1=bias2_sb[:], op=ALU.add)
         nc.gpsimd.tensor_scalar(
             out=bias_share[:], in0=bias_share[:], scalar1=1.0 / NH, scalar2=0.0, op0=ALU.mult, op1=ALU.add
         )
-        summands = keep.tile([P, COL_TILES, NH], BF16)
-        shift_sb = keep.tile([P, COL_TILES], F32)
-        for t in range(COL_TILES):
+        summands = keep.tile([P, W2_ROWS, NH], BF16)
+        shift_sb = keep.tile([P, W2_ROWS], F32)
+        for i in range(W2_ROWS):
             nc.scalar.activation(
-                out=summands[:, t],
-                in_=w2_sb[:, t],
+                out=summands[:, i],
+                in_=w2_sb[:, i],
                 func=ACT.Identity,
                 scale=float(NH),
-                bias=bias_share[:, t : t + 1],
-                accum_out=shift_sb[:, t : t + 1],
+                bias=bias_share[:, i : i + 1],
+                accum_out=shift_sb[:, i : i + 1],
             )
 
         total = keep.tile([P, ROW_TILES, N], F32)
@@ -180,16 +184,16 @@ def tile_advresnet_s_kernel(tc, x, y, beta, bias_lin, W1, W2, bias1, bias2, adv,
             )
         for r in range(ROW_TILES):
             nc.vector.tensor_tensor(out=total[:, r], in0=total[:, r], in1=acc[r][:], op=ALU.add)
-        shift_rows = psum.tile([P, COL_TILES, P], F32)
-        for t in range(COL_TILES):
+        shift_rows = psum.tile([P, W2_ROWS, P], F32)
+        for i in range(W2_ROWS):
             nc.tensor.transpose(
-                shift_rows[:, t, :],
-                shift_sb[:, t : t + 1].to_broadcast([P, P]),
+                shift_rows[:, i, :],
+                shift_sb[:, i : i + 1].to_broadcast([P, P]),
                 ident[:],
             )
         for r in range(ROW_TILES):
-            total_qt = total[:, r].rearrange("p (q t) -> p q t", t=COL_TILES)
+            total_qi = total[:, r].rearrange("p (q i) -> p q i", i=W2_ROWS)
             nc.vector.tensor_tensor(
-                out=total_qt, in0=total_qt, in1=shift_rows[:].rearrange("p t q -> p q t"), op=ALU.add
+                out=total_qi, in0=total_qi, in1=shift_rows[:].rearrange("p i q -> p q i"), op=ALU.add
             )
             nc.sync.dma_start(out=out[r * P : (r + 1) * P, :], in_=total[:, r])

from contextlib import ExitStack

import concourse.mybir as mybir
from concourse.masks import make_identity

F32 = mybir.dt.float32
BF16 = mybir.dt.bfloat16
U32 = mybir.dt.uint32
U8 = mybir.dt.uint8
FP8X4 = mybir.dt.float8_e4m3fn_x4
ALU = mybir.AluOpType
ACT = mybir.ActivationFunctionType
AXIS = mybir.AxisListType

P = 128
PACK = 4
PAIR = 2
HALVES = PACK // PAIR
K_PASS = P * PACK
B, K, N, NH = 256, 1024, 512, 512
PASSES = K // K_PASS
ROW_TILES = B // P
COL_TILES = N // P
W2_ROWS = N // P
RUN = 4
EPSILON = 0.1

VECTOR_COLS = 256

FLOPS = 2 * B * K * N
BYTES = 2 * (B * K + B * N + K * N + N * NH + 2 * N) + 4 * B * N


def tile_advresnet_s_kernel(tc, x, y, beta, bias_lin, W1, W2, bias1, bias2, adv, out):
    assert adv == 1
    nc = tc.nc
    with ExitStack() as ctx:
        keep = ctx.enter_context(tc.tile_pool(name="keep", bufs=1))
        psum = ctx.enter_context(tc.psum_pool(name="psum", bufs=1))
        ctx.enter_context(tc.manual_schedule())

        beta_sb = keep.tile([P, PASSES, PACK, N], BF16)
        for g in range(PASSES):
            for u in range(HALVES):
                first_row = g * K_PASS + u * PAIR * P
                nc.sync.dma_start(
                    out=beta_sb[:, g, PAIR * u : PAIR * (u + 1), :].rearrange("p e n -> p (e n)"),
                    in_=beta[first_row : first_row + PAIR * P, :].rearrange("(p e) n -> p (e n)", e=PAIR),
                )
        x_sb = keep.tile([P, ROW_TILES * K], BF16)
        nc.sync.dma_start(
            out=x_sb[:].rearrange("p (r k) -> p r k", r=ROW_TILES),
            in_=x.rearrange("(r p) k -> p r k", p=P),
        )
        w2_sb = keep.tile([P, W2_ROWS, NH], BF16)
        nc.sync.dma_start(out=w2_sb[:], in_=W2.rearrange("(p i) h -> p i h", p=P))
        y_sb = keep.tile([P, ROW_TILES, N], BF16)
        nc.sync.dma_start(out=y_sb[:], in_=y.rearrange("(r p) n -> p r n", p=P))
        bias_lin_sb = keep.tile([P, W2_ROWS], BF16)
        bias2_sb = keep.tile([P, W2_ROWS], BF16)
        nc.scalar.dma_start(out=bias_lin_sb[:], in_=bias_lin.rearrange("(p i) -> p i", p=P))
        nc.scalar.dma_start(out=bias2_sb[:], in_=bias2.rearrange("(p i) -> p i", p=P))

        ident = keep.tile([P, P], F32)
        make_identity(nc, ident[:])
        weight = keep.tile([P, 2], BF16)
        nc.vector.memset(weight[:, 0:1], -1.0)
        nc.vector.memset(weight[:, 1:2], 2.0)

        beta_pos = keep.tile([P, PASSES, PACK, N], BF16)
        beta_grouped = keep.tile([P, PASSES, N, PACK], BF16, align_bytes=64)
        norm_ps = psum.tile([P, COL_TILES, 2 * PASSES], F32)
        for g in range(PASSES):
            for u in range(HALVES):
                nc.vector.tensor_scalar_max(
                    out=beta_pos[:, g, PAIR * u : PAIR * (u + 1), :],
                    in0=beta_sb[:, g, PAIR * u : PAIR * (u + 1), :],
                    scalar1=0.0,
                )
            src = beta_sb[:, g].rearrange("p t (c i) -> p c t i", i=RUN)
            dst = beta_grouped[:, g].rearrange("p (c i) t -> p c t i", i=RUN)
            cut = VECTOR_COLS // RUN
            nc.vector.tensor_copy(out=dst[:, :cut], in_=src[:, :cut])
            nc.scalar.copy(out=dst[:, cut:], in_=src[:, cut:])
            for part, source in enumerate((beta_sb, beta_pos)):
                for j in range(COL_TILES):
                    for t in range(PACK):
                        nc.tensor.matmul(
                            out=norm_ps[:, j, 2 * g + part : 2 * g + part + 1],
                            lhsT=source[:, g, t, j * P : (j + 1) * P],
                            rhs=weight[:, part : part + 1],
                            start=(t == 0),
                            stop=(t == PACK - 1),
                        )

        beta_codes = keep.tile([P, PASSES, N], U32, align_bytes=64)
        beta_scales = keep.tile([P, PASSES, N], U8, align_bytes=64)
        norm_sb = keep.tile([P, COL_TILES], F32)

        def quantise_beta(g):
            nc.vector.quantize_mx(
                out=beta_codes[:, g].bitcast(FP8X4),
                scales=beta_scales[:, g],
                in_=beta_grouped[:, g].rearrange("p n t -> p (n t)"),
            )

        quantise_beta(0)
        nc.vector.tensor_reduce(out=norm_sb[:], in_=norm_ps[:], axis=AXIS.X, op=ALU.add)
        quantise_beta(1)

        x_words = x_sb[:].bitcast(F32).rearrange("p (r w) -> p r w", r=ROW_TILES)
        x_grouped = keep.tile([P, PASSES * B * PACK], BF16, align_bytes=64)
        x_grouped_words = x_grouped[:].bitcast(F32).rearrange(
            "p (g row u) -> p g row u", g=PASSES, u=HALVES
        )
        x_codes = keep.tile([P, PASSES * B], U32, align_bytes=64)
        x_scales = keep.tile([P, PASSES * B], U8, align_bytes=64)
        for g in range(PASSES):
            xt = psum.tile([P, HALVES, B], F32, name="xt%d" % g)
            for u in range(HALVES):
                for r in range(ROW_TILES):
                    first_word = (HALVES * g + u) * P
                    nc.tensor.transpose(
                        xt[:, u, r * P : (r + 1) * P],
                        x_words[:, r, first_word : first_word + P],
                        ident[:],
                    )
            nc.scalar.copy(out=x_grouped_words[:, g], in_=xt[:].rearrange("p u row -> p row u"))
        for g in range(PASSES):
            nc.vector.quantize_mx(
                out=x_codes[:, g * B : (g + 1) * B].bitcast(FP8X4),
                scales=x_scales[:, g * B : (g + 1) * B],
                in_=x_grouped[:, g * B * PACK : (g + 1) * B * PACK],
            )

        norm_rows = psum.tile([P, N], F32)
        for j in range(COL_TILES):
            nc.tensor.transpose(
                norm_rows[:, j * P : (j + 1) * P],
                norm_sb[:, j : j + 1].to_broadcast([P, P]),
                ident[:],
            )

        acc = [psum.tile([P, N], F32, name="acc%d" % r) for r in range(ROW_TILES)]
        for g in range(PASSES):
            for r in range(ROW_TILES):
                rows = slice(g * B + r * P, g * B + (r + 1) * P)
                nc.tensor.matmul_mx(
                    out=acc[r][:],
                    lhsT=x_codes[:, rows].bitcast(FP8X4),
                    lhsT_scale=x_scales[:, rows],
                    rhs=beta_codes[:, g].bitcast(FP8X4),
                    rhs_scale=beta_scales[:, g],
                    start=(g == 0),
                    stop=(g == PASSES - 1),
                )

        bias_share = keep.tile([P, W2_ROWS], F32)
        nc.gpsimd.tensor_tensor(out=bias_share[:], in0=bias_lin_sb[:], in1=bias2_sb[:], op=ALU.add)
        nc.gpsimd.tensor_scalar(
            out=bias_share[:], in0=bias_share[:], scalar1=1.0 / NH, scalar2=0.0, op0=ALU.mult, op1=ALU.add
        )
        summands = keep.tile([P, W2_ROWS, NH], BF16)
        shift_sb = keep.tile([P, W2_ROWS], F32)
        for i in range(W2_ROWS):
            nc.scalar.activation(
                out=summands[:, i],
                in_=w2_sb[:, i],
                func=ACT.Identity,
                scale=float(NH),
                bias=bias_share[:, i : i + 1],
                accum_out=shift_sb[:, i : i + 1],
            )

        total = keep.tile([P, ROW_TILES, N], F32)
        for r in range(ROW_TILES):
            nc.vector.scalar_tensor_tensor(
                out=total[:, r],
                in0=y_sb[:, r],
                scalar=-EPSILON,
                in1=norm_rows[:],
                op0=ALU.mult,
                op1=ALU.mult,
            )
        for r in range(ROW_TILES):
            nc.vector.tensor_tensor(out=total[:, r], in0=total[:, r], in1=acc[r][:], op=ALU.add)
        shift_rows = psum.tile([P, W2_ROWS, P], F32)
        for i in range(W2_ROWS):
            nc.tensor.transpose(
                shift_rows[:, i, :],
                shift_sb[:, i : i + 1].to_broadcast([P, P]),
                ident[:],
            )
        for r in range(ROW_TILES):
            total_qi = total[:, r].rearrange("p (q i) -> p q i", i=W2_ROWS)
            nc.vector.tensor_tensor(
                out=total_qi, in0=total_qi, in1=shift_rows[:].rearrange("p i q -> p q i"), op=ALU.add
            )
            nc.sync.dma_start(out=out[r * P : (r + 1) * P, :], in_=total[:, r])
